import numpy as np
import ml_dtypes


def mxq(x, axis, fmt="e4m3"):
    dtype, down = {"e4m3": (ml_dtypes.float8_e4m3fn, 7), "e5m2": (ml_dtypes.float8_e5m2, 14)}[fmt]
    v = np.moveaxis(np.asarray(x, np.float32).astype(ml_dtypes.bfloat16).astype(np.float64), axis, -1)
    blocks = v.reshape(v.shape[:-1] + (-1, 32))
    amax = np.abs(blocks).max(-1, keepdims=True)
    byte = np.maximum(np.where(amax > 0, np.frexp(amax)[1] - 1 + 127, 0) - down, 1)
    scale = np.exp2(byte - 127.0)
    codes = (blocks / scale).astype(np.float32).astype(dtype).astype(np.float64)
    return np.moveaxis((codes * scale).reshape(v.shape), -1, axis)


WIDE = False


def mx_kscale(k):
    if not WIDE:
        return np.ones(k)
    levels = np.array([10, -10, 5, -5, 0])
    a = np.random.permutation(np.resize(levels, k // 512 * 4)).reshape(k // 512, 4)
    idx = np.arange(k)
    return np.exp2(a[idx // 512, idx % 128 // 32])


BF16 = ml_dtypes.bfloat16


def bf(x):
    return np.asarray(x, np.float32).astype(BF16)


def f64(x):
    return np.asarray(x).astype(np.float64)


N, DIN, H1, H2, C, NC, G = 1024, 512, 512, 256, 128, 512, 8


def setup_inputs():
    s, t = mx_kscale(N), mx_kscale(DIN)
    return {"F_": bf(np.random.uniform(size=(N, N)) * 2.0 / np.sqrt(N) * s),
            "X": bf(np.random.standard_normal((N, DIN)) / s[:, None] * t),
            "W1": bf(np.random.standard_normal((DIN, H1)) * 0.8 / np.sqrt(DIN) / t[:, None]),
            "b1": bf(np.random.standard_normal(H1) * 0.3)}


def reference(F_, X, W1, b1):
    agg = mxq(f64(F_), 1, "e4m3") @ mxq(f64(X), 0, "e4m3")
    return np.tanh((mxq(agg, 1, "e4m3") @ mxq(f64(W1), 0, "e4m3")) + f64(b1))

@@ -1,0 +1,162 @@
+from contextlib import ExitStack
+
+import concourse.mybir as mybir
+from concourse.masks import make_identity
+
+F32 = mybir.dt.float32
+BF16 = mybir.dt.bfloat16
+U32 = mybir.dt.uint32
+U8 = mybir.dt.uint8
+FP8X4 = mybir.dt.float8_e4m3fn_x4
+
+P = 128
+PACK = 4
+K_PASS = P * PACK
+NODES = 1024
+FEATS = 512
+HIDDEN = 512
+BLOCKS = NODES // P
+PASSES = NODES // K_PASS
+FEAT_TILES = FEATS // P
+LOAD_BLOCKS = 2
+
+FLOPS = 2 * NODES * NODES * FEATS + 2 * NODES * FEATS * HIDDEN
+
+
+def tile_controencodnet_pa_kernel(tc, F_, X, W1, b1, out):
+    nc = tc.nc
+    with ExitStack() as ctx:
+        keep = ctx.enter_context(tc.tile_pool(name="keep", bufs=1))
+        psum_f = ctx.enter_context(tc.psum_pool(name="psum_f", bufs=3))
+        psum_a = ctx.enter_context(tc.psum_pool(name="psum_a", bufs=2))
+        psum_o = ctx.enter_context(tc.psum_pool(name="psum_o", bufs=3))
+
+        f_in = keep.tile([P, BLOCKS, NODES], BF16)
+        x_in = keep.tile([P, PASSES, PACK, FEATS], BF16)
+        w_in = keep.tile([P, PACK, HIDDEN], BF16)
+        f_grouped = keep.tile([P, BLOCKS, PASSES * P * PACK], BF16, align_bytes=64)
+        x_grouped = keep.tile([P, PASSES, FEATS, PACK], BF16, align_bytes=64)
+        w_grouped = keep.tile([P, HIDDEN, PACK], BF16, align_bytes=64)
+        a_grouped = keep.tile([P, BLOCKS, P, PACK], BF16, align_bytes=64)
+        f_codes = keep.tile([P, BLOCKS, PASSES * P], U32, align_bytes=64)
+        f_scales = keep.tile([P, BLOCKS, PASSES * P], U8, align_bytes=64)
+        x_codes = keep.tile([P, PASSES, FEATS], U32, align_bytes=64)
+        x_scales = keep.tile([P, PASSES, FEATS], U8, align_bytes=64)
+        w_codes = keep.tile([P, HIDDEN], U32, align_bytes=64)
+        w_scales = keep.tile([P, HIDDEN], U8, align_bytes=64)
+        a_codes = keep.tile([P, BLOCKS, P], U32, align_bytes=64)
+        a_scales = keep.tile([P, BLOCKS, P], U8, align_bytes=64)
+        result = keep.tile([P, BLOCKS, HIDDEN], F32)
+
+        identity = keep.tile([P, P], F32)
+        ones = keep.tile([P, P], BF16)
+        bias_row = keep.tile([P, HIDDEN], BF16)
+        bias_all = keep.tile([P, HIDDEN], F32)
+        warm = keep.tile([P, 1], F32)
+
+        f_rows = F_.rearrange("(n r) k -> n r k", r=BLOCKS)
+        out_rows = out.rearrange("(n r) c -> n r c", r=BLOCKS)
+
+        x_rows = X.rearrange("(g u p e) c -> g u p e c", g=PASSES, u=2, p=P, e=2)
+        for g in range(PASSES):
+            for u in range(2):
+                nc.sync.dma_start(out=x_in[:, g, 2 * u : 2 * u + 2, :], in_=x_rows[g, u])
+
+        def load_f(first):
+            blocks = slice(first, first + LOAD_BLOCKS)
+            nc.sync.dma_start(out=f_in[:, blocks, :], in_=f_rows[:, blocks, :])
+
+        load_f(0)
+        nc.sync.dma_start(out=w_in[:], in_=W1.rearrange("(t p) c -> p t c", p=P))
+        for first in range(LOAD_BLOCKS, BLOCKS, LOAD_BLOCKS):
+            load_f(first)
+
+        nc.vector.memset(warm[:], 0.0)
+        nc.scalar.activation(out=warm[:], in_=warm[:], func=mybir.ActivationFunctionType.Tanh)
+        make_identity(nc, identity[:])
+        nc.gpsimd.memset(ones[:], 1.0)
+        nc.gpsimd.memset(bias_row[:], 0.0)
+        nc.scalar.dma_start(out=bias_row[0:1, :], in_=b1.rearrange("(o c) -> o c", o=1))
+
+        def regroup(grouped, rows):
+            nc.vector.tensor_copy(
+                out=grouped.rearrange("p (c i) t -> p c t i", i=4),
+                in_=rows.rearrange("p t (c i) -> p c t i", i=4),
+            )
+
+        def quantise(codes, scales, grouped):
+            nc.vector.quantize_mx(out=codes.bitcast(FP8X4), scales=scales, in_=grouped)
+
+        def spread_bias():
+            bank = psum_o.tile([P, HIDDEN], F32, tag="o")
+            nc.tensor.matmul(out=bank[:], lhsT=ones[:], rhs=bias_row[:], start=True, stop=True)
+            nc.vector.tensor_copy(out=bias_all[:], in_=bank[:])
+
+        def transpose_f(r):
+            words = f_in[:, r, :].bitcast(F32)
+            bank = psum_f.tile([P, PASSES * 2, P], F32, tag="f")
+            for j in range(PASSES * 2):
+                nc.tensor.transpose(bank[:, j, :], words[:, j * P : (j + 1) * P], identity[:])
+            nc.scalar.copy(
+                out=f_grouped[:, r, :].bitcast(F32).rearrange("p (g n u) -> p g n u", g=PASSES, u=2),
+                in_=bank[:].rearrange("p (g u) n -> p g n u", u=2),
+            )
+            quantise(f_codes[:, r, :], f_scales[:, r, :], f_grouped[:, r, :])
+
+        def aggregate(r):
+            bank = psum_a.tile([P, FEAT_TILES, P], F32, tag="a")
+            for t in range(FEAT_TILES):
+                feats = slice(t * P, (t + 1) * P)
+                for g in range(PASSES):
+                    nodes = slice(g * P, (g + 1) * P)
+                    nc.tensor.matmul_mx(
+                        out=bank[:, t, :],
+                        lhsT=x_codes[:, g, feats].bitcast(FP8X4),
+                        lhsT_scale=x_scales[:, g, feats],
+                        rhs=f_codes[:, r, nodes].bitcast(FP8X4),
+                        rhs_scale=f_scales[:, r, nodes],
+                        start=(g == 0),
+                        stop=(g == PASSES - 1),
+                    )
+            nc.scalar.copy(out=a_grouped[:, r], in_=bank[:].rearrange("p t n -> p n t"))
+            quantise(
+                a_codes[:, r, :], a_scales[:, r, :], a_grouped[:, r].rearrange("p n t -> p (n t)")
+            )
+
+        def project(r):
+            bank = psum_o.tile([P, HIDDEN], F32, tag="o")
+            nc.tensor.matmul_mx(
+                out=bank[:],
+                lhsT=a_codes[:, r, :].bitcast(FP8X4),
+                lhsT_scale=a_scales[:, r, :],
+                rhs=w_codes[:].bitcast(FP8X4),
+                rhs_scale=w_scales[:],
+                start=True,
+                stop=True,
+            )
+            nc.vector.tensor_tensor(
+                out=result[:, r, :], in0=bank[:], in1=bias_all[:], op=mybir.AluOpType.add
+            )
+            nc.scalar.activation(
+                out=result[:, r, :], in_=result[:, r, :], func=mybir.ActivationFunctionType.Tanh
+            )
+            nc.sync.dma_start(out=out_rows[:, r, :], in_=result[:, r, :])
+
+        for g in range(PASSES):
+            regroup(x_grouped[:, g], x_in[:, g])
+        for g in range(PASSES):
+            quantise(
+                x_codes[:, g, :], x_scales[:, g, :], x_grouped[:, g].rearrange("p c t -> p (c t)")
+            )
+
+        for step in range(BLOCKS + 2):
+            if step < BLOCKS:
+                transpose_f(step)
+            if step == 0:
+                regroup(w_grouped[:], w_in[:])
+                quantise(w_codes[:], w_scales[:], w_grouped[:].rearrange("p c t -> p (c t)"))
+                spread_bias()
+            if 1 <= step <= BLOCKS:
+                aggregate(step - 1)
+            if step >= 2:
+                project(step - 2)

@@ -18,7 +18,10 @@ HIDDEN = 512
 BLOCKS = NODES // P
 PASSES = NODES // K_PASS
 FEAT_TILES = FEATS // P
-LOAD_BLOCKS = 2
+GROUP = 2
+GROUPS = BLOCKS // GROUP
+AGG_LAG = 1
+OUT_LAG = 3
 
 FLOPS = 2 * NODES * NODES * FEATS + 2 * NODES * FEATS * HIDDEN
 
@@ -27,9 +30,10 @@ def tile_controencodnet_pa_kernel(tc, F_, X, W1, b1, out):
     nc = tc.nc
     with ExitStack() as ctx:
         keep = ctx.enter_context(tc.tile_pool(name="keep", bufs=1))
-        psum_f = ctx.enter_context(tc.psum_pool(name="psum_f", bufs=3))
-        psum_a = ctx.enter_context(tc.psum_pool(name="psum_a", bufs=2))
-        psum_o = ctx.enter_context(tc.psum_pool(name="psum_o", bufs=3))
+        psum_f = ctx.enter_context(tc.psum_pool(name="psum_f", bufs=2 * GROUP))
+        psum_a = ctx.enter_context(tc.psum_pool(name="psum_a", bufs=GROUP))
+        psum_o = ctx.enter_context(tc.psum_pool(name="psum_o", bufs=GROUP))
+        ctx.enter_context(tc.manual_schedule())
 
         f_in = keep.tile([P, BLOCKS, NODES], BF16)
         x_in = keep.tile([P, PASSES, PACK, FEATS], BF16)
@@ -62,21 +66,22 @@ def tile_controencodnet_pa_kernel(tc, F_, X, W1, b1, out):
             for u in range(2):
                 nc.sync.dma_start(out=x_in[:, g, 2 * u : 2 * u + 2, :], in_=x_rows[g, u])
 
-        def load_f(first):
-            blocks = slice(first, first + LOAD_BLOCKS)
+        def load_f(group):
+            blocks = slice(group * GROUP, (group + 1) * GROUP)
             nc.sync.dma_start(out=f_in[:, blocks, :], in_=f_rows[:, blocks, :])
 
         load_f(0)
+        load_f(1)
         nc.sync.dma_start(out=w_in[:], in_=W1.rearrange("(t p) c -> p t c", p=P))
-        for first in range(LOAD_BLOCKS, BLOCKS, LOAD_BLOCKS):
-            load_f(first)
+        for group in range(2, GROUPS):
+            load_f(group)
 
+        nc.gpsimd.memset(bias_row[:], 0.0)
+        nc.scalar.dma_start(out=bias_row[0:1, :], in_=b1.rearrange("(o c) -> o c", o=1))
         nc.vector.memset(warm[:], 0.0)
         nc.scalar.activation(out=warm[:], in_=warm[:], func=mybir.ActivationFunctionType.Tanh)
         make_identity(nc, identity[:])
         nc.gpsimd.memset(ones[:], 1.0)
-        nc.gpsimd.memset(bias_row[:], 0.0)
-        nc.scalar.dma_start(out=bias_row[0:1, :], in_=b1.rearrange("(o c) -> o c", o=1))
 
         def regroup(grouped, rows):
             nc.vector.tensor_copy(
@@ -92,14 +97,19 @@ def tile_controencodnet_pa_kernel(tc, F_, X, W1, b1, out):
             nc.tensor.matmul(out=bank[:], lhsT=ones[:], rhs=bias_row[:], start=True, stop=True)
             nc.vector.tensor_copy(out=bias_all[:], in_=bank[:])
 
+        f_banks = {}
+
         def transpose_f(r):
             words = f_in[:, r, :].bitcast(F32)
             bank = psum_f.tile([P, PASSES * 2, P], F32, tag="f")
             for j in range(PASSES * 2):
                 nc.tensor.transpose(bank[:, j, :], words[:, j * P : (j + 1) * P], identity[:])
+            f_banks[r] = bank
+
+        def quantise_f(r):
             nc.scalar.copy(
                 out=f_grouped[:, r, :].bitcast(F32).rearrange("p (g n u) -> p g n u", g=PASSES, u=2),
-                in_=bank[:].rearrange("p (g u) n -> p g n u", u=2),
+                in_=f_banks[r][:].rearrange("p (g u) n -> p g n u", u=2),
             )
             quantise(f_codes[:, r, :], f_scales[:, r, :], f_grouped[:, r, :])
 
@@ -137,10 +147,17 @@ def tile_controencodnet_pa_kernel(tc, F_, X, W1, b1, out):
             nc.vector.tensor_tensor(
                 out=result[:, r, :], in0=bank[:], in1=bias_all[:], op=mybir.AluOpType.add
             )
+
+        def finish(r):
             nc.scalar.activation(
                 out=result[:, r, :], in_=result[:, r, :], func=mybir.ActivationFunctionType.Tanh
             )
             nc.sync.dma_start(out=out_rows[:, r, :], in_=result[:, r, :])
+
+        def blocks_of(group):
+            if 0 <= group < GROUPS:
+                return range(group * GROUP, (group + 1) * GROUP)
+            return range(0)
 
         for g in range(PASSES):
             regroup(x_grouped[:, g], x_in[:, g])
@@ -149,14 +166,18 @@ def tile_controencodnet_pa_kernel(tc, F_, X, W1, b1, out):
                 x_codes[:, g, :], x_scales[:, g, :], x_grouped[:, g].rearrange("p c t -> p (c t)")
             )
 
-        for step in range(BLOCKS + 2):
-            if step < BLOCKS:
-                transpose_f(step)
-            if step == 0:
+        for step in range(GROUPS + OUT_LAG):
+            for r in blocks_of(step):
+                transpose_f(r)
+            for r in blocks_of(step - OUT_LAG):
+                project(r)
+            for r in blocks_of(step):
+                quantise_f(r)
+            for r in blocks_of(step - AGG_LAG):
+                aggregate(r)
+            for r in blocks_of(step - OUT_LAG):
+                finish(r)
+            if step == AGG_LAG:
                 regroup(w_grouped[:], w_in[:])
                 quantise(w_codes[:], w_scales[:], w_grouped[:].rearrange("p c t -> p (c t)"))
                 spread_bias()
-            if 1 <= step <= BLOCKS:
-                aggregate(step - 1)
-            if step >= 2:
-                project(step - 2)

@@ -62,26 +62,25 @@ def tile_controencodnet_pa_kernel(tc, F_, X, W1, b1, out):
         out_rows = out.rearrange("(n r) c -> n r c", r=BLOCKS)
 
         x_rows = X.rearrange("(g u p e) c -> g u p e c", g=PASSES, u=2, p=P, e=2)
+        def load_f(first, count):
+            blocks = slice(first, first + count)
+            nc.sync.dma_start(out=f_in[:, blocks, :], in_=f_rows[:, blocks, :])
+
         for g in range(PASSES):
             for u in range(2):
                 nc.sync.dma_start(out=x_in[:, g, 2 * u : 2 * u + 2, :], in_=x_rows[g, u])
-
-        def load_f(group):
-            blocks = slice(group * GROUP, (group + 1) * GROUP)
-            nc.sync.dma_start(out=f_in[:, blocks, :], in_=f_rows[:, blocks, :])
-
-        load_f(0)
-        load_f(1)
+            load_f(g, 1)
+        load_f(PASSES, GROUP)
         nc.sync.dma_start(out=w_in[:], in_=W1.rearrange("(t p) c -> p t c", p=P))
-        for group in range(2, GROUPS):
-            load_f(group)
+        for first in range(PASSES + GROUP, BLOCKS, GROUP):
+            load_f(first, GROUP)
 
-        nc.gpsimd.memset(bias_row[:], 0.0)
+        nc.vector.memset(bias_row[:], 0.0)
         nc.scalar.dma_start(out=bias_row[0:1, :], in_=b1.rearrange("(o c) -> o c", o=1))
+        nc.vector.memset(ones[:], 1.0)
         nc.vector.memset(warm[:], 0.0)
         nc.scalar.activation(out=warm[:], in_=warm[:], func=mybir.ActivationFunctionType.Tanh)
         make_identity(nc, identity[:])
-        nc.gpsimd.memset(ones[:], 1.0)
 
         def regroup(grouped, rows):
             nc.vector.tensor_copy(
@@ -95,7 +94,7 @@ def tile_controencodnet_pa_kernel(tc, F_, X, W1, b1, out):
         def spread_bias():
             bank = psum_o.tile([P, HIDDEN], F32, tag="o")
             nc.tensor.matmul(out=bank[:], lhsT=ones[:], rhs=bias_row[:], start=True, stop=True)
-            nc.vector.tensor_copy(out=bias_all[:], in_=bank[:])
+            nc.scalar.copy(out=bias_all[:], in_=bank[:])
 
         f_banks = {}
 
@@ -128,7 +127,10 @@ def tile_controencodnet_pa_kernel(tc, F_, X, W1, b1, out):
                         start=(g == 0),
                         stop=(g == PASSES - 1),
                     )
-            nc.scalar.copy(out=a_grouped[:, r], in_=bank[:].rearrange("p t n -> p n t"))
+            if r < BLOCKS - 1:
+                nc.scalar.copy(out=a_grouped[:, r], in_=bank[:].rearrange("p t n -> p n t"))
+            else:
+                nc.vector.tensor_copy(out=a_grouped[:, r], in_=bank[:].rearrange("p t n -> p n t"))
             quantise(
                 a_codes[:, r, :], a_scales[:, r, :], a_grouped[:, r].rearrange("p n t -> p (n t)")
             )
@@ -161,7 +163,6 @@ def tile_controencodnet_pa_kernel(tc, F_, X, W1, b1, out):
 
         for g in range(PASSES):
             regroup(x_grouped[:, g], x_in[:, g])
-        for g in range(PASSES):
             quantise(
                 x_codes[:, g, :], x_scales[:, g, :], x_grouped[:, g].rearrange("p c t -> p (c t)")
             )
@@ -173,6 +174,8 @@ def tile_controencodnet_pa_kernel(tc, F_, X, W1, b1, out):
                 project(r)
             for r in blocks_of(step):
                 quantise_f(r)
+            if step == 0:
+                spread_bias()
             for r in blocks_of(step - AGG_LAG):
                 aggregate(r)
             for r in blocks_of(step - OUT_LAG):
@@ -180,4 +183,3 @@ def tile_controencodnet_pa_kernel(tc, F_, X, W1, b1, out):
             if step == AGG_LAG:
                 regroup(w_grouped[:], w_in[:])
                 quantise(w_codes[:], w_scales[:], w_grouped[:].rearrange("p c t -> p (c t)"))
-                spread_bias()

@@ -88,6 +88,10 @@ def tile_controencodnet_pa_kernel(tc, F_, X, W1, b1, out):
                 in_=rows.rearrange("p t (c i) -> p c t i", i=4),
             )
 
+        def regroup_w(half):
+            cols = slice(half * (HIDDEN // 2), (half + 1) * (HIDDEN // 2))
+            regroup(w_grouped[:, cols, :], w_in[:, :, cols])
+
         def quantise(codes, scales, grouped):
             nc.vector.quantize_mx(out=codes.bitcast(FP8X4), scales=scales, in_=grouped)
 
@@ -112,6 +116,8 @@ def tile_controencodnet_pa_kernel(tc, F_, X, W1, b1, out):
             )
             quantise(f_codes[:, r, :], f_scales[:, r, :], f_grouped[:, r, :])
 
+        a_banks = {}
+
         def aggregate(r):
             bank = psum_a.tile([P, FEAT_TILES, P], F32, tag="a")
             for t in range(FEAT_TILES):
@@ -127,10 +133,16 @@ def tile_controencodnet_pa_kernel(tc, F_, X, W1, b1, out):
                         start=(g == 0),
                         stop=(g == PASSES - 1),
                     )
+            a_banks[r] = bank
+
+        def round_agg(r):
+            hopping = a_banks[r][:].rearrange("p t n -> p n t")
             if r < BLOCKS - 1:
-                nc.scalar.copy(out=a_grouped[:, r], in_=bank[:].rearrange("p t n -> p n t"))
+                nc.scalar.copy(out=a_grouped[:, r], in_=hopping)
             else:
-                nc.vector.tensor_copy(out=a_grouped[:, r], in_=bank[:].rearrange("p t n -> p n t"))
+                nc.vector.tensor_copy(out=a_grouped[:, r], in_=hopping)
+
+        def quantise_agg(r):
             quantise(
                 a_codes[:, r, :], a_scales[:, r, :], a_grouped[:, r].rearrange("p n t -> p (n t)")
             )
@@ -176,10 +188,16 @@ def tile_controencodnet_pa_kernel(tc, F_, X, W1, b1, out):
                 quantise_f(r)
             if step == 0:
                 spread_bias()
+            if step == AGG_LAG:
+                regroup_w(0)
             for r in blocks_of(step - AGG_LAG):
                 aggregate(r)
+            for r in blocks_of(step - AGG_LAG):
+                round_agg(r)
+            for r in blocks_of(step - AGG_LAG):
+                quantise_agg(r)
             for r in blocks_of(step - OUT_LAG):
                 finish(r)
             if step == AGG_LAG:
-                regroup(w_grouped[:], w_in[:])
+                regroup_w(1)
                 quantise(w_codes[:], w_scales[:], w_grouped[:].rearrange("p c t -> p (c t)"))

from contextlib import ExitStack

import concourse.mybir as mybir
from concourse.masks import make_identity

F32 = mybir.dt.float32
BF16 = mybir.dt.bfloat16
U32 = mybir.dt.uint32
U8 = mybir.dt.uint8
FP8X4 = mybir.dt.float8_e4m3fn_x4

P = 128
PACK = 4
K_PASS = P * PACK
NODES = 1024
FEATS = 512
HIDDEN = 512
BLOCKS = NODES // P
PASSES = NODES // K_PASS
FEAT_TILES = FEATS // P
GROUP = 2
GROUPS = BLOCKS // GROUP
AGG_LAG = 1
OUT_LAG = 3

FLOPS = 2 * NODES * NODES * FEATS + 2 * NODES * FEATS * HIDDEN


def tile_controencodnet_pa_kernel(tc, F_, X, W1, b1, out):
    nc = tc.nc
    with ExitStack() as ctx:
        keep = ctx.enter_context(tc.tile_pool(name="keep", bufs=1))
        psum_f = ctx.enter_context(tc.psum_pool(name="psum_f", bufs=2 * GROUP))
        psum_a = ctx.enter_context(tc.psum_pool(name="psum_a", bufs=GROUP))
        psum_o = ctx.enter_context(tc.psum_pool(name="psum_o", bufs=GROUP))
        ctx.enter_context(tc.manual_schedule())

        f_in = keep.tile([P, BLOCKS, NODES], BF16)
        x_in = keep.tile([P, PASSES, PACK, FEATS], BF16)
        w_in = keep.tile([P, PACK, HIDDEN], BF16)
        f_grouped = keep.tile([P, BLOCKS, PASSES * P * PACK], BF16, align_bytes=64)
        x_grouped = keep.tile([P, PASSES, FEATS, PACK], BF16, align_bytes=64)
        w_grouped = keep.tile([P, HIDDEN, PACK], BF16, align_bytes=64)
        a_grouped = keep.tile([P, BLOCKS, P, PACK], BF16, align_bytes=64)
        f_codes = keep.tile([P, BLOCKS, PASSES * P], U32, align_bytes=64)
        f_scales = keep.tile([P, BLOCKS, PASSES * P], U8, align_bytes=64)
        x_codes = keep.tile([P, PASSES, FEATS], U32, align_bytes=64)
        x_scales = keep.tile([P, PASSES, FEATS], U8, align_bytes=64)
        w_codes = keep.tile([P, HIDDEN], U32, align_bytes=64)
        w_scales = keep.tile([P, HIDDEN], U8, align_bytes=64)
        a_codes = keep.tile([P, BLOCKS, P], U32, align_bytes=64)
        a_scales = keep.tile([P, BLOCKS, P], U8, align_bytes=64)
        result = keep.tile([P, BLOCKS, HIDDEN], F32)

        identity = keep.tile([P, P], F32)
        ones = keep.tile([P, P], BF16)
        bias_row = keep.tile([P, HIDDEN], BF16)
        bias_all = keep.tile([P, HIDDEN], F32)
        warm = keep.tile([P, 1], F32)

        f_rows = F_.rearrange("(n r) k -> n r k", r=BLOCKS)
        out_rows = out.rearrange("(n r) c -> n r c", r=BLOCKS)

        x_rows = X.rearrange("(g u p e) c -> g u p e c", g=PASSES, u=2, p=P, e=2)
        def load_f(first, count):
            blocks = slice(first, first + count)
            nc.sync.dma_start(out=f_in[:, blocks, :], in_=f_rows[:, blocks, :])

        for g in range(PASSES):
            for u in range(2):
                nc.sync.dma_start(out=x_in[:, g, 2 * u : 2 * u + 2, :], in_=x_rows[g, u])
            load_f(g, 1)
        load_f(PASSES, GROUP)
        nc.sync.dma_start(out=w_in[:], in_=W1.rearrange("(t p) c -> p t c", p=P))
        for first in range(PASSES + GROUP, BLOCKS, GROUP):
            load_f(first, GROUP)

        nc.vector.memset(bias_row[:], 0.0)
        nc.scalar.dma_start(out=bias_row[0:1, :], in_=b1.rearrange("(o c) -> o c", o=1))
        nc.vector.memset(ones[:], 1.0)
        nc.vector.memset(warm[:], 0.0)
        nc.scalar.activation(out=warm[:], in_=warm[:], func=mybir.ActivationFunctionType.Tanh)
        make_identity(nc, identity[:])

        def regroup(grouped, rows):
            nc.vector.tensor_copy(
                out=grouped.rearrange("p (c i) t -> p c t i", i=4),
                in_=rows.rearrange("p t (c i) -> p c t i", i=4),
            )

        def regroup_w(half):
            cols = slice(half * (HIDDEN // 2), (half + 1) * (HIDDEN // 2))
            regroup(w_grouped[:, cols, :], w_in[:, :, cols])

        def quantise(codes, scales, grouped):
            nc.vector.quantize_mx(out=codes.bitcast(FP8X4), scales=scales, in_=grouped)

        def spread_bias():
            bank = psum_o.tile([P, HIDDEN], F32, tag="o")
            nc.tensor.matmul(out=bank[:], lhsT=ones[:], rhs=bias_row[:], start=True, stop=True)
            nc.scalar.copy(out=bias_all[:], in_=bank[:])

        f_banks = {}

        def transpose_f(r):
            words = f_in[:, r, :].bitcast(F32)
            bank = psum_f.tile([P, PASSES * 2, P], F32, tag="f")
            for j in range(PASSES * 2):
                nc.tensor.transpose(bank[:, j, :], words[:, j * P : (j + 1) * P], identity[:])
            f_banks[r] = bank

        def quantise_f(r):
            nc.scalar.copy(
                out=f_grouped[:, r, :].bitcast(F32).rearrange("p (g n u) -> p g n u", g=PASSES, u=2),
                in_=f_banks[r][:].rearrange("p (g u) n -> p g n u", u=2),
            )
            quantise(f_codes[:, r, :], f_scales[:, r, :], f_grouped[:, r, :])

        a_banks = {}

        def aggregate(r):
            bank = psum_a.tile([P, FEAT_TILES, P], F32, tag="a")
            for t in range(FEAT_TILES):
                feats = slice(t * P, (t + 1) * P)
                for g in range(PASSES):
                    nodes = slice(g * P, (g + 1) * P)
                    nc.tensor.matmul_mx(
                        out=bank[:, t, :],
                        lhsT=x_codes[:, g, feats].bitcast(FP8X4),
                        lhsT_scale=x_scales[:, g, feats],
                        rhs=f_codes[:, r, nodes].bitcast(FP8X4),
                        rhs_scale=f_scales[:, r, nodes],
                        start=(g == 0),
                        stop=(g == PASSES - 1),
                    )
            a_banks[r] = bank

        def round_agg(r):
            hopping = a_banks[r][:].rearrange("p t n -> p n t")
            if r < BLOCKS - 1:
                nc.scalar.copy(out=a_grouped[:, r], in_=hopping)
            else:
                nc.vector.tensor_copy(out=a_grouped[:, r], in_=hopping)

        def quantise_agg(r):
            quantise(
                a_codes[:, r, :], a_scales[:, r, :], a_grouped[:, r].rearrange("p n t -> p (n t)")
            )

        def project(r):
            bank = psum_o.tile([P, HIDDEN], F32, tag="o")
            nc.tensor.matmul_mx(
                out=bank[:],
                lhsT=a_codes[:, r, :].bitcast(FP8X4),
                lhsT_scale=a_scales[:, r, :],
                rhs=w_codes[:].bitcast(FP8X4),
                rhs_scale=w_scales[:],
                start=True,
                stop=True,
            )
            nc.vector.tensor_tensor(
                out=result[:, r, :], in0=bank[:], in1=bias_all[:], op=mybir.AluOpType.add
            )

        def finish(r):
            nc.scalar.activation(
                out=result[:, r, :], in_=result[:, r, :], func=mybir.ActivationFunctionType.Tanh
            )
            nc.sync.dma_start(out=out_rows[:, r, :], in_=result[:, r, :])

        def blocks_of(group):
            if 0 <= group < GROUPS:
                return range(group * GROUP, (group + 1) * GROUP)
            return range(0)

        for g in range(PASSES):
            regroup(x_grouped[:, g], x_in[:, g])
            quantise(
                x_codes[:, g, :], x_scales[:, g, :], x_grouped[:, g].rearrange("p c t -> p (c t)")
            )

        for step in range(GROUPS + OUT_LAG):
            for r in blocks_of(step):
                transpose_f(r)
            for r in blocks_of(step - OUT_LAG):
                project(r)
            for r in blocks_of(step):
                quantise_f(r)
            if step == 0:
                spread_bias()
            if step == AGG_LAG:
                regroup_w(0)
            for r in blocks_of(step - AGG_LAG):
                aggregate(r)
            for r in blocks_of(step - AGG_LAG):
                round_agg(r)
            for r in blocks_of(step - AGG_LAG):
                quantise_agg(r)
            for r in blocks_of(step - OUT_LAG):
                finish(r)
            if step == AGG_LAG:
                regroup_w(1)
                quantise(w_codes[:], w_scales[:], w_grouped[:].rearrange("p c t -> p (c t)"))
